import numpy as np
import ml_dtypes

BF16 = ml_dtypes.bfloat16


def bf(x):
    return np.asarray(x, np.float32).astype(BF16)


def f32(x):
    return np.asarray(x, np.float32)


def f64(x):
    return np.asarray(x).astype(np.float64)


def striped(idx):
    return np.tile(idx.reshape(-1, 16).T, (8, 1))


D, D3, T, NH, DH, S, RUN, K, N, P = 1024, 3072, 512, 8, 128, 512, 256, 4, 1024, 128
QK_SCALE, V_SCALE, BIAS_SCALE, EMB_SCALE, MASK_NEG = 0.3, 2.0, 0.15, 0.5, -30.0


def setup_inputs():
    x = bf(np.random.standard_normal((D, T)))
    col = np.concatenate([np.full(D, QK_SCALE), np.full(D, QK_SCALE), np.full(D, V_SCALE)]) / np.sqrt(D)
    w_qkv = bf(np.random.standard_normal((D, D3)) * col[None, :])
    w_fc = bf(np.random.standard_normal((D, D)) / np.sqrt(D))
    rb = bf(BIAS_SCALE * np.random.standard_normal((DH, NH)))
    wb = bf(BIAS_SCALE * np.random.standard_normal((DH, NH)))
    r_emb = f32(EMB_SCALE * np.random.standard_normal((DH, S)))
    u = np.arange(T)[:, None]
    t = np.arange(T)[None, :]
    mask = f32(np.where((u <= t) | (u < P), 0.0, MASK_NEG))
    idx = np.concatenate([np.random.permutation(S)[:RUN] for _ in range(K)])
    return {"x": x, "w_qkv": w_qkv, "w_fc": w_fc, "rb": rb, "wb": wb, "r_emb": r_emb, "mask": mask, "offs": striped(idx)}


def reference(x, w_qkv, w_fc, rb, wb, r_emb, mask, offs):
    idx = offs[:16].T.reshape(-1)
    qkv = f64(w_qkv).T @ f64(x)
    q = qkv[:D].reshape(NH, DH, T)
    key = qkv[D:D + D].reshape(NH, DH, T)
    val = qkv[D + D:].reshape(NH, DH, T)
    sq = (q * f64(rb).T[:, :, None]).sum(axis=1)
    sk = (key * f64(wb).T[:, :, None]).sum(axis=1)
    sc = np.concatenate([sq, sk], axis=1)
    rel = f64(r_emb)[:, idx][None, :, :] * sc[:, None, :]
    a = q + rel[:, :, :T]
    kr = rel[:, :, T:]
    scores = a.transpose(0, 2, 1) @ key + q.transpose(0, 2, 1) @ kr + f64(mask).T[None, :, :]
    e = np.exp(scores - scores.max(axis=2, keepdims=True))
    attn = e / e.sum(axis=2, keepdims=True)
    o = (val @ attn.transpose(0, 2, 1)).reshape(D, T)
    return f64(w_fc).T @ o

@@ -1,0 +1,167 @@
+import concourse.mybir as mybir
+from concourse.masks import make_identity
+
+BF16, F32, U16 = mybir.dt.bfloat16, mybir.dt.float32, mybir.dt.uint16
+ADD, MULT, MAX = mybir.AluOpType.add, mybir.AluOpType.mult, mybir.AluOpType.max
+EXP = mybir.ActivationFunctionType.Exp
+AXIS_X = mybir.AxisListType.X
+
+P = 128
+D = 1024
+T = 512
+NH = 8
+KB = D // P
+TB = T // P
+CH = 512
+HPC = CH // P
+NLIST = 1024
+
+FLOPS = 2 * D * 3 * D * T + 2 * P * NH * NLIST + 3 * 2 * NH * T * T * P + 2 * D * D * T
+
+
+def tile_relativemultiheadattention_b_kernel(tc, x, w_qkv, w_fc, rb, wb, r_emb, mask, offs, out):
+    nc = tc.nc
+    with (
+        tc.tile_pool(name="held", bufs=1) as held,
+        tc.tile_pool(name="per_head", bufs=2) as per_head,
+        tc.tile_pool(name="per_block", bufs=3) as per_block,
+        tc.tile_pool(name="stats", bufs=4) as stats,
+        tc.psum_pool(name="psum_acc", bufs=3) as psum_acc,
+        tc.psum_pool(name="psum_scores", bufs=3) as psum_scores,
+        tc.psum_pool(name="psum_flip", bufs=2) as psum_flip,
+    ):
+        offsets = held.tile([P, NLIST // 16], U16, name="offsets")
+        nc.sync.dma_start(offsets[:], offs)
+
+        x_sb = [held.tile([P, T], BF16, name=f"x{a}") for a in range(KB)]
+        w_sb = [[[held.tile([P, CH], BF16, name=f"w{part}{c}{a}") for a in range(KB)]
+                 for c in range(NH // HPC)] for part in range(3)]
+
+        def load_w(queue, part, c):
+            col = part * D + c * CH
+            for a in range(KB):
+                queue.dma_start(w_sb[part][c][a][:], w_qkv[a * P:(a + 1) * P, col:col + CH])
+
+        for a in range(KB):
+            nc.sync.dma_start(x_sb[a][:], x[a * P:(a + 1) * P, :])
+        load_w(nc.scalar, 0, 0)
+        load_w(nc.sync, 1, 0)
+
+        rb_sb = held.tile([P, NH], BF16, name="rb_sb")
+        wb_sb = held.tile([P, NH], BF16, name="wb_sb")
+        table = held.tile([P, T], F32, name="table")
+        mask_sb = [held.tile([P, T], F32, name=f"mask{ub}") for ub in range(TB)]
+        nc.gpsimd.dma_start(rb_sb[:], rb)
+        nc.gpsimd.dma_start(wb_sb[:], wb)
+        nc.gpsimd.dma_start(table[:], r_emb)
+        for ub in range(TB):
+            nc.gpsimd.dma_start(mask_sb[ub][:], mask[ub * P:(ub + 1) * P, :])
+
+        load_w(nc.scalar, 2, 0)
+        load_w(nc.sync, 0, 1)
+        load_w(nc.scalar, 1, 1)
+        load_w(nc.sync, 2, 1)
+        wfc_sb = [held.tile([P, D], BF16, name=f"wfc{h}") for h in range(NH)]
+        for h in range(NH):
+            nc.gpsimd.dma_start(wfc_sb[h][:], w_fc[h * P:(h + 1) * P, :])
+
+        ident_f32 = held.tile([P, P], F32, name="ident_f32")
+        ident_bf = held.tile([P, P], BF16, name="ident_bf")
+        make_identity(nc, ident_f32[:])
+        make_identity(nc, ident_bf[:])
+        rb_wide = held.tile([P, NH, P], BF16, name="rb_wide")
+        wb_wide = held.tile([P, NH, P], BF16, name="wb_wide")
+        nc.vector.tensor_copy(rb_wide[:], rb_sb[:].unsqueeze(2).to_broadcast([P, NH, P]))
+        nc.vector.tensor_copy(wb_wide[:], wb_sb[:].unsqueeze(2).to_broadcast([P, NH, P]))
+
+        mask_t = [held.tile([P, T], F32, name=f"mask_t{tb}") for tb in range(TB)]
+        for tb in range(TB):
+            flipped = psum_scores.tile([P, T], F32, name="flipped", tag="scores")
+            for ub in range(TB):
+                nc.tensor.transpose(flipped[:, ub * P:(ub + 1) * P],
+                                    mask_sb[ub][:, tb * P:(tb + 1) * P], ident_f32[:])
+            nc.vector.tensor_copy(mask_t[tb][:], flipped[:])
+
+        q_bf = [held.tile([P, T], BF16, name=f"q{h}") for h in range(NH)]
+        k_bf = [held.tile([P, T], BF16, name=f"k{h}") for h in range(NH)]
+        val_t = [[held.tile([P, CH], BF16, name=f"val_t{c}{ub}") for ub in range(TB)]
+                 for c in range(NH // HPC)]
+        o_bf = [held.tile([P, T], BF16, name=f"o{h}") for h in range(NH)]
+
+        def project_head(part, h, dest):
+            pieces = w_sb[part][h // HPC]
+            col = (h % HPC) * P
+            acc = psum_acc.tile([P, T], F32, name="acc", tag="acc")
+            for a in range(KB):
+                nc.tensor.matmul(acc[:], lhsT=pieces[a][:, col:col + P], rhs=x_sb[a][:],
+                                 start=(a == 0), stop=(a == KB - 1))
+            nc.scalar.copy(dest[:], acc[:])
+
+        def project_values(c):
+            for ub in range(TB):
+                acc = psum_acc.tile([P, CH], F32, name="acc", tag="acc")
+                for a in range(KB):
+                    nc.tensor.matmul(acc[:], lhsT=x_sb[a][:, ub * P:(ub + 1) * P], rhs=w_sb[2][c][a][:],
+                                     start=(a == 0), stop=(a == KB - 1))
+                nc.scalar.copy(val_t[c][ub][:], acc[:])
+
+        def relative_term(h, wide, operand, first_column, name):
+            acc = psum_acc.tile([P, T], F32, name="acc", tag="acc")
+            nc.tensor.matmul(acc[:], lhsT=wide[:, h, :], rhs=operand[:], start=True, stop=True)
+            sc = per_head.tile([P, T], F32, name="sc_" + name, tag="sc_" + name)
+            nc.scalar.copy(sc[:], acc[:])
+            rel = per_head.tile([P, T], F32, name="rel_" + name, tag="rel_" + name)
+            picked = table[:].indirect(offsets[:, first_column:first_column + T // 16])
+            nc.vector.tensor_tensor(rel[:], picked, sc[:], MULT)
+            return rel
+
+        for h in range(NH):
+            project_head(0, h, q_bf[h])
+            project_head(1, h, k_bf[h])
+
+            rel_q = relative_term(h, rb_wide, q_bf[h], 0, "q")
+            rel_k = relative_term(h, wb_wide, k_bf[h], T // 16, "k")
+            a_bf = per_head.tile([P, T], BF16, name="a_bf", tag="a_bf")
+            kr_bf = per_head.tile([P, T], BF16, name="kr_bf", tag="kr_bf")
+            nc.gpsimd.tensor_tensor(a_bf[:], rel_q[:], q_bf[h][:], ADD)
+            nc.gpsimd.tensor_scalar(kr_bf[:], rel_k[:], 1.0, 0.0, MULT, ADD)
+
+            attn_t = per_head.tile([P, TB, T], BF16, name="attn_t", tag="attn_t")
+            for tb in range(TB):
+                block = slice(tb * P, (tb + 1) * P)
+                scores_ps = psum_scores.tile([P, T], F32, name="scores_ps", tag="scores")
+                nc.tensor.matmul(scores_ps[:], lhsT=a_bf[:, block], rhs=k_bf[h][:], start=True, stop=False)
+                nc.tensor.matmul(scores_ps[:], lhsT=q_bf[h][:, block], rhs=kr_bf[:], start=False, stop=True)
+                scores = per_block.tile([P, T], F32, name="scores", tag="scores_sb")
+                nc.vector.tensor_tensor(scores[:], scores_ps[:], mask_t[tb][:], ADD)
+                neg_max = stats.tile([P, 1], F32, name="neg_max", tag="neg_max")
+                nc.vector.tensor_reduce(neg_max[:], scores[:], AXIS_X, MAX, negate=True)
+                expd = per_block.tile([P, T], F32, name="expd", tag="expd")
+                row_sum = stats.tile([P, 1], F32, name="row_sum", tag="row_sum")
+                nc.scalar.activation(expd[:], scores[:], EXP, bias=neg_max[:], scale=1.0, accum_out=row_sum[:])
+                inv_sum = stats.tile([P, 1], F32, name="inv_sum", tag="inv_sum")
+                nc.vector.reciprocal(inv_sum[:], row_sum[:])
+                attn = per_block.tile([P, T], BF16, name="attn", tag="attn")
+                nc.gpsimd.tensor_scalar(attn[:], expd[:], inv_sum[:], 0.0, MULT, ADD)
+                flip = psum_flip.tile([P, TB, P], BF16, name="flip", tag="flip")
+                for ub in range(TB):
+                    nc.tensor.transpose(flip[:, ub, :], attn[:, ub * P:(ub + 1) * P], ident_bf[:])
+                nc.scalar.copy(attn_t[:, :, block], flip[:])
+
+            if h % HPC == 0:
+                project_values(h // HPC)
+            o_ps = psum_acc.tile([P, T], F32, name="o_ps", tag="acc")
+            for ub in range(TB):
+                col = (h % HPC) * P
+                nc.tensor.matmul(o_ps[:], lhsT=val_t[h // HPC][ub][:, col:col + P], rhs=attn_t[:, ub, :],
+                                 start=(ub == 0), stop=(ub == TB - 1))
+            nc.scalar.copy(o_bf[h][:], o_ps[:])
+
+        for m in range(D // P):
+            acc = psum_acc.tile([P, T], F32, name="acc", tag="acc")
+            for h in range(NH):
+                nc.tensor.matmul(acc[:], lhsT=wfc_sb[h][:, m * P:(m + 1) * P], rhs=o_bf[h][:],
+                                 start=(h == 0), stop=(h == NH - 1))
+            out_sb = per_block.tile([P, T], F32, name="out_sb", tag="out_sb")
+            nc.scalar.copy(out_sb[:], acc[:])
+            nc.sync.dma_start(out[m * P:(m + 1) * P, :], out_sb[:])

@@ -15,6 +15,10 @@ TB = T // P
 CH = 512
 HPC = CH // P
 NLIST = 1024
+Q, K, V = 0, 1, 2
+STEPS = NH * TB
+FLIP_LAG = 2
+VALUES_LAG = TB + FLIP_LAG + 1
 
 FLOPS = 2 * D * 3 * D * T + 2 * P * NH * NLIST + 3 * 2 * NH * T * T * P + 2 * D * D * T
 
@@ -26,9 +30,8 @@ def tile_relativemultiheadattention_b_kernel(tc, x, w_qkv, w_fc, rb, wb, r_emb, 
         tc.tile_pool(name="per_head", bufs=2) as per_head,
         tc.tile_pool(name="per_block", bufs=3) as per_block,
         tc.tile_pool(name="stats", bufs=4) as stats,
-        tc.psum_pool(name="psum_acc", bufs=3) as psum_acc,
-        tc.psum_pool(name="psum_scores", bufs=3) as psum_scores,
-        tc.psum_pool(name="psum_flip", bufs=2) as psum_flip,
+        tc.psum_pool(name="banks", bufs=6) as banks,
+        tc.psum_pool(name="flips", bufs=2) as flips,
     ):
         offsets = held.tile([P, NLIST // 16], U16, name="offsets")
         nc.sync.dma_start(offsets[:], offs)
@@ -37,34 +40,29 @@ def tile_relativemultiheadattention_b_kernel(tc, x, w_qkv, w_fc, rb, wb, r_emb, 
         w_sb = [[[held.tile([P, CH], BF16, name=f"w{part}{c}{a}") for a in range(KB)]
                  for c in range(NH // HPC)] for part in range(3)]
 
-        def load_w(queue, part, c):
+        def load_w(part, c, a):
             col = part * D + c * CH
-            for a in range(KB):
-                queue.dma_start(w_sb[part][c][a][:], w_qkv[a * P:(a + 1) * P, col:col + CH])
+            nc.scalar.dma_start(w_sb[part][c][a][:], w_qkv[a * P:(a + 1) * P, col:col + CH])
 
         for a in range(KB):
             nc.sync.dma_start(x_sb[a][:], x[a * P:(a + 1) * P, :])
-        load_w(nc.scalar, 0, 0)
-        load_w(nc.sync, 1, 0)
+            load_w(Q, 0, a)
+            load_w(K, 0, a)
 
         rb_sb = held.tile([P, NH], BF16, name="rb_sb")
         wb_sb = held.tile([P, NH], BF16, name="wb_sb")
         table = held.tile([P, T], F32, name="table")
         mask_sb = [held.tile([P, T], F32, name=f"mask{ub}") for ub in range(TB)]
-        nc.gpsimd.dma_start(rb_sb[:], rb)
-        nc.gpsimd.dma_start(wb_sb[:], wb)
-        nc.gpsimd.dma_start(table[:], r_emb)
+        nc.sync.dma_start(rb_sb[:], rb)
+        nc.sync.dma_start(wb_sb[:], wb)
+        nc.sync.dma_start(table[:], r_emb)
         for ub in range(TB):
-            nc.gpsimd.dma_start(mask_sb[ub][:], mask[ub * P:(ub + 1) * P, :])
-
-        load_w(nc.scalar, 2, 0)
-        load_w(nc.sync, 0, 1)
-        load_w(nc.scalar, 1, 1)
-        load_w(nc.sync, 2, 1)
+            nc.sync.dma_start(mask_sb[ub][:], mask[ub * P:(ub + 1) * P, :])
         wfc_sb = [held.tile([P, D], BF16, name=f"wfc{h}") for h in range(NH)]
-        for h in range(NH):
-            nc.gpsimd.dma_start(wfc_sb[h][:], w_fc[h * P:(h + 1) * P, :])
 
+        warm = held.tile([P, 1], F32, name="warm")
+        nc.vector.memset(warm[:], 0.0)
+        nc.scalar.activation(warm[:], warm[:], EXP)
         ident_f32 = held.tile([P, P], F32, name="ident_f32")
         ident_bf = held.tile([P, P], BF16, name="ident_bf")
         make_identity(nc, ident_f32[:])
@@ -74,94 +72,177 @@ def tile_relativemultiheadattention_b_kernel(tc, x, w_qkv, w_fc, rb, wb, r_emb, 
         nc.vector.tensor_copy(rb_wide[:], rb_sb[:].unsqueeze(2).to_broadcast([P, NH, P]))
         nc.vector.tensor_copy(wb_wide[:], wb_sb[:].unsqueeze(2).to_broadcast([P, NH, P]))
 
-        mask_t = [held.tile([P, T], F32, name=f"mask_t{tb}") for tb in range(TB)]
-        for tb in range(TB):
-            flipped = psum_scores.tile([P, T], F32, name="flipped", tag="scores")
-            for ub in range(TB):
-                nc.tensor.transpose(flipped[:, ub * P:(ub + 1) * P],
-                                    mask_sb[ub][:, tb * P:(tb + 1) * P], ident_f32[:])
-            nc.vector.tensor_copy(mask_t[tb][:], flipped[:])
-
-        q_bf = [held.tile([P, T], BF16, name=f"q{h}") for h in range(NH)]
-        k_bf = [held.tile([P, T], BF16, name=f"k{h}") for h in range(NH)]
+        qk_bf = [[held.tile([P, T], BF16, name=f"qk{part}{h}") for h in range(NH)] for part in (Q, K)]
         val_t = [[held.tile([P, CH], BF16, name=f"val_t{c}{ub}") for ub in range(TB)]
                  for c in range(NH // HPC)]
         o_bf = [held.tile([P, T], BF16, name=f"o{h}") for h in range(NH)]
+        out_sb = [held.tile([P, T], F32, name=f"out_sb{m}") for m in range(D // P)]
+        mask_t = [held.tile([P, T], F32, name=f"mask_t{tb}") for tb in range(TB)]
 
-        def project_head(part, h, dest):
-            pieces = w_sb[part][h // HPC]
+        def project_head(part, h):
             col = (h % HPC) * P
-            acc = psum_acc.tile([P, T], F32, name="acc", tag="acc")
+            acc = banks.tile([P, T], F32, name="acc", tag="bank")
             for a in range(KB):
-                nc.tensor.matmul(acc[:], lhsT=pieces[a][:, col:col + P], rhs=x_sb[a][:],
+                nc.tensor.matmul(acc[:], lhsT=w_sb[part][h // HPC][a][:, col:col + P], rhs=x_sb[a][:],
                                  start=(a == 0), stop=(a == KB - 1))
-            nc.scalar.copy(dest[:], acc[:])
+            nc.scalar.copy(qk_bf[part][h][:], acc[:])
 
-        def project_values(c):
-            for ub in range(TB):
-                acc = psum_acc.tile([P, CH], F32, name="acc", tag="acc")
-                for a in range(KB):
-                    nc.tensor.matmul(acc[:], lhsT=x_sb[a][:, ub * P:(ub + 1) * P], rhs=w_sb[2][c][a][:],
-                                     start=(a == 0), stop=(a == KB - 1))
-                nc.scalar.copy(val_t[c][ub][:], acc[:])
+        def project_values(c, ub):
+            acc = banks.tile([P, CH], F32, name="acc", tag="bank")
+            for a in range(KB):
+                nc.tensor.matmul(acc[:], lhsT=x_sb[a][:, ub * P:(ub + 1) * P], rhs=w_sb[V][c][a][:],
+                                 start=(a == 0), stop=(a == KB - 1))
+            nc.scalar.copy(val_t[c][ub][:], acc[:])
 
-        def relative_term(h, wide, operand, first_column, name):
-            acc = psum_acc.tile([P, T], F32, name="acc", tag="acc")
-            nc.tensor.matmul(acc[:], lhsT=wide[:, h, :], rhs=operand[:], start=True, stop=True)
-            sc = per_head.tile([P, T], F32, name="sc_" + name, tag="sc_" + name)
-            nc.scalar.copy(sc[:], acc[:])
-            rel = per_head.tile([P, T], F32, name="rel_" + name, tag="rel_" + name)
-            picked = table[:].indirect(offsets[:, first_column:first_column + T // 16])
-            nc.vector.tensor_tensor(rel[:], picked, sc[:], MULT)
+        def project_output(m, heads):
+            acc = banks.tile([P, T], F32, name="acc", tag="bank")
+            for h in heads:
+                nc.tensor.matmul(acc[:], lhsT=wfc_sb[h][:, m * P:(m + 1) * P], rhs=o_bf[h][:],
+                                 start=(h == heads[0]), stop=(h == heads[-1]))
+            if heads[0] == 0:
+                nc.scalar.copy(out_sb[m][:], acc[:])
+            else:
+                nc.vector.tensor_tensor(out_sb[m][:], acc[:], out_sb[m][:], ADD)
+
+        sc = [[None, None] for h in range(NH)]
+        a_bf = [None] * NH
+        kr_bf = [None] * NH
+
+        def scalars(h):
+            for part, wide in ((Q, rb_wide), (K, wb_wide)):
+                acc = banks.tile([P, T], F32, name="acc", tag="bank")
+                nc.tensor.matmul(acc[:], lhsT=wide[:, h, :], rhs=qk_bf[part][h][:], start=True, stop=True)
+                sc[h][part] = per_head.tile([P, T], F32, name=f"sc{part}", tag=f"sc{part}")
+                nc.scalar.copy(sc[h][part][:], acc[:])
+
+        def look_up(h, part):
+            first = part * (T // 16)
+            rel = per_head.tile([P, T], F32, name=f"rel{part}", tag=f"rel{part}")
+            picked = table[:].indirect(offsets[:, first:first + T // 16])
+            nc.vector.tensor_tensor(rel[:], picked, sc[h][part][:], MULT)
             return rel
 
-        for h in range(NH):
-            project_head(0, h, q_bf[h])
-            project_head(1, h, k_bf[h])
+        def query_side(h):
+            rel = look_up(h, Q)
+            a_bf[h] = per_head.tile([P, T], BF16, name="a_bf", tag="a_bf")
+            nc.gpsimd.tensor_tensor(a_bf[h][:], rel[:], qk_bf[Q][h][:], ADD)
 
-            rel_q = relative_term(h, rb_wide, q_bf[h], 0, "q")
-            rel_k = relative_term(h, wb_wide, k_bf[h], T // 16, "k")
-            a_bf = per_head.tile([P, T], BF16, name="a_bf", tag="a_bf")
-            kr_bf = per_head.tile([P, T], BF16, name="kr_bf", tag="kr_bf")
-            nc.gpsimd.tensor_tensor(a_bf[:], rel_q[:], q_bf[h][:], ADD)
-            nc.gpsimd.tensor_scalar(kr_bf[:], rel_k[:], 1.0, 0.0, MULT, ADD)
+        def key_side(h):
+            rel = look_up(h, K)
+            kr_bf[h] = per_head.tile([P, T], BF16, name="kr_bf", tag="kr_bf")
+            nc.vector.tensor_copy(kr_bf[h][:], rel[:])
 
-            attn_t = per_head.tile([P, TB, T], BF16, name="attn_t", tag="attn_t")
-            for tb in range(TB):
-                block = slice(tb * P, (tb + 1) * P)
-                scores_ps = psum_scores.tile([P, T], F32, name="scores_ps", tag="scores")
-                nc.tensor.matmul(scores_ps[:], lhsT=a_bf[:, block], rhs=k_bf[h][:], start=True, stop=False)
-                nc.tensor.matmul(scores_ps[:], lhsT=q_bf[h][:, block], rhs=kr_bf[:], start=False, stop=True)
-                scores = per_block.tile([P, T], F32, name="scores", tag="scores_sb")
-                nc.vector.tensor_tensor(scores[:], scores_ps[:], mask_t[tb][:], ADD)
-                neg_max = stats.tile([P, 1], F32, name="neg_max", tag="neg_max")
-                nc.vector.tensor_reduce(neg_max[:], scores[:], AXIS_X, MAX, negate=True)
-                expd = per_block.tile([P, T], F32, name="expd", tag="expd")
-                row_sum = stats.tile([P, 1], F32, name="row_sum", tag="row_sum")
-                nc.scalar.activation(expd[:], scores[:], EXP, bias=neg_max[:], scale=1.0, accum_out=row_sum[:])
-                inv_sum = stats.tile([P, 1], F32, name="inv_sum", tag="inv_sum")
-                nc.vector.reciprocal(inv_sum[:], row_sum[:])
-                attn = per_block.tile([P, T], BF16, name="attn", tag="attn")
-                nc.gpsimd.tensor_scalar(attn[:], expd[:], inv_sum[:], 0.0, MULT, ADD)
-                flip = psum_flip.tile([P, TB, P], BF16, name="flip", tag="flip")
-                for ub in range(TB):
-                    nc.tensor.transpose(flip[:, ub, :], attn[:, ub * P:(ub + 1) * P], ident_bf[:])
-                nc.scalar.copy(attn_t[:, :, block], flip[:])
+        expd = [None] * STEPS
+        row_sum = [None] * STEPS
+        attn = [None] * STEPS
+        attn_t = [None] * NH
 
-            if h % HPC == 0:
-                project_values(h // HPC)
-            o_ps = psum_acc.tile([P, T], F32, name="o_ps", tag="acc")
+        def scores_and_exp(n):
+            h, tb = divmod(n, TB)
+            block = slice(tb * P, (tb + 1) * P)
+            scores_ps = banks.tile([P, T], F32, name="scores_ps", tag="bank")
+            nc.tensor.matmul(scores_ps[:], lhsT=a_bf[h][:, block], rhs=qk_bf[K][h][:], start=True, stop=False)
+            nc.tensor.matmul(scores_ps[:], lhsT=qk_bf[Q][h][:, block], rhs=kr_bf[h][:], start=False, stop=True)
+            scores = per_block.tile([P, T], F32, name="scores", tag="scores")
+            nc.vector.tensor_tensor(scores[:], scores_ps[:], mask_t[tb][:], ADD)
+            neg_max = stats.tile([P, 1], F32, name="neg_max", tag="neg_max")
+            nc.vector.tensor_reduce(neg_max[:], scores[:], AXIS_X, MAX, negate=True)
+            expd[n] = per_block.tile([P, T], F32, name="expd", tag="expd")
+            row_sum[n] = stats.tile([P, 1], F32, name="row_sum", tag="row_sum")
+            nc.scalar.activation(expd[n][:], scores[:], EXP, bias=neg_max[:], scale=1.0, accum_out=row_sum[n][:])
+
+        def normalise(n):
+            inv_sum = stats.tile([P, 1], F32, name="inv_sum", tag="inv_sum")
+            nc.vector.reciprocal(inv_sum[:], row_sum[n][:])
+            attn[n] = per_block.tile([P, T], BF16, name="attn", tag="attn")
+            nc.gpsimd.tensor_scalar(attn[n][:], expd[n][:], inv_sum[:], 0.0, MULT, ADD)
+
+        def flip(n):
+            h, tb = divmod(n, TB)
+            if tb == 0:
+                attn_t[h] = per_head.tile([P, TB, T], BF16, name="attn_t", tag="attn_t")
+            flipped = flips.tile([P, TB, P], BF16, name="flipped", tag="flipped")
             for ub in range(TB):
-                col = (h % HPC) * P
-                nc.tensor.matmul(o_ps[:], lhsT=val_t[h // HPC][ub][:, col:col + P], rhs=attn_t[:, ub, :],
+                nc.tensor.transpose(flipped[:, ub, :], attn[n][:, ub * P:(ub + 1) * P], ident_bf[:])
+            nc.scalar.copy(attn_t[h][:, :, tb * P:(tb + 1) * P], flipped[:])
+
+        def meet_values(h):
+            col = (h % HPC) * P
+            o_ps = banks.tile([P, T], F32, name="o_ps", tag="bank")
+            for ub in range(TB):
+                nc.tensor.matmul(o_ps[:], lhsT=val_t[h // HPC][ub][:, col:col + P], rhs=attn_t[h][:, ub, :],
                                  start=(ub == 0), stop=(ub == TB - 1))
             nc.scalar.copy(o_bf[h][:], o_ps[:])
 
+        first_four = [(part, h) for h in (0, 1) for part in (Q, K)]
+        accs = [banks.tile([P, T], F32, name=f"acc{part}{h}", tag="bank") for part, h in first_four]
+        for a in range(KB):
+            for acc, (part, h) in zip(accs, first_four):
+                nc.tensor.matmul(acc[:], lhsT=w_sb[part][0][a][:, h * P:(h + 1) * P], rhs=x_sb[a][:],
+                                 start=(a == 0), stop=(a == KB - 1))
+        for acc, (part, h) in zip(accs, first_four):
+            if part == Q:
+                nc.scalar.copy(qk_bf[part][h][:], acc[:])
+            else:
+                nc.vector.tensor_copy(qk_bf[part][h][:], acc[:])
+
+        ahead = [(project_head, (part, h)) for h in (2, 3) for part in (Q, K)]
+        ahead += [(project_values, (0, ub)) for ub in range(TB)]
+        ahead += [(project_head, (part, h)) for h in range(HPC, NH) for part in (Q, K)]
+        ahead += [(project_values, (1, ub)) for ub in range(TB)]
+
+        scalars(0)
+        for a in range(KB):
+            load_w(V, 0, a)
+        project_head(*ahead[0][1])
+        query_side(0)
+        key_side(0)
+        for tb in range(TB):
+            flipped = banks.tile([P, T], F32, name="mask_flipped", tag="bank")
+            for ub in range(TB):
+                nc.tensor.transpose(flipped[:, ub * P:(ub + 1) * P],
+                                    mask_sb[ub][:, tb * P:(tb + 1) * P], ident_f32[:])
+            nc.scalar.copy(mask_t[tb][:], flipped[:])
+        project_head(*ahead[1][1])
+        ahead = ahead[2:]
+
+        first_output_step = TB * (HPC - 1) + VALUES_LAG + 1
+        shares = [[0, 1, 2, 3], [4, 5], [6, 7]]
+
+        for n in range(STEPS + VALUES_LAG - TB + 1):
+            h, tb = divmod(n, TB)
+            if n == 0:
+                for a in range(KB):
+                    load_w(Q, 1, a)
+                    load_w(K, 1, a)
+            if n == TB:
+                for a in range(KB):
+                    load_w(V, 1, a)
+                for g in range(NH):
+                    nc.scalar.dma_start(wfc_sb[g][:], w_fc[g * P:(g + 1) * P, :])
+
+            if 1 <= n <= STEPS:
+                normalise(n - 1)
+            if n < STEPS:
+                scores_and_exp(n)
+            if h + 1 < NH:
+                if tb == 0:
+                    scalars(h + 1)
+                if tb == 1:
+                    query_side(h + 1)
+                if tb == 2:
+                    key_side(h + 1)
+            if n < len(ahead):
+                work, args = ahead[n]
+                work(*args)
+            if n >= first_output_step:
+                share, m = divmod(n - first_output_step, D // P)
+                project_output(m, shares[share])
+            if 0 <= n - FLIP_LAG < STEPS:
+                flip(n - FLIP_LAG)
+            if n >= VALUES_LAG and (n - VALUES_LAG) % TB == 0:
+                meet_values((n - VALUES_LAG) // TB)
+
         for m in range(D // P):
-            acc = psum_acc.tile([P, T], F32, name="acc", tag="acc")
-            for h in range(NH):
-                nc.tensor.matmul(acc[:], lhsT=wfc_sb[h][:, m * P:(m + 1) * P], rhs=o_bf[h][:],
-                                 start=(h == 0), stop=(h == NH - 1))
-            out_sb = per_block.tile([P, T], F32, name="out_sb", tag="out_sb")
-            nc.scalar.copy(out_sb[:], acc[:])
-            nc.sync.dma_start(out[m * P:(m + 1) * P, :], out_sb[:])
+            project_output(m, shares[2])
+            nc.sync.dma_start(out[m * P:(m + 1) * P, :], out_sb[m][:])

@@ -11,6 +11,7 @@ D = 1024
 T = 512
 NH = 8
 KB = D // P
+MB = D // P
 TB = T // P
 CH = 512
 HPC = CH // P
@@ -36,29 +37,37 @@ def tile_relativemultiheadattention_b_kernel(tc, x, w_qkv, w_fc, rb, wb, r_emb, 
         offsets = held.tile([P, NLIST // 16], U16, name="offsets")
         nc.sync.dma_start(offsets[:], offs)
 
-        x_sb = [held.tile([P, T], BF16, name=f"x{a}") for a in range(KB)]
-        w_sb = [[[held.tile([P, CH], BF16, name=f"w{part}{c}{a}") for a in range(KB)]
-                 for c in range(NH // HPC)] for part in range(3)]
+        x_rows = x.rearrange("(a p) t -> p a t", p=P)
+        w_rows = w_qkv.rearrange("(a p) r -> p a r", p=P)
 
-        def load_w(part, c, a):
-            col = part * D + c * CH
-            nc.scalar.dma_start(w_sb[part][c][a][:], w_qkv[a * P:(a + 1) * P, col:col + CH])
+        def load_blocks(queue, rows, first_col, first_block, count, name):
+            piece = held.tile([P, count, CH], BF16, name=f"{name}_{first_block}")
+            queue.dma_start(piece[:], rows[:, first_block:first_block + count, first_col:first_col + CH])
+            return [piece[:, i, :] for i in range(count)]
 
-        for a in range(KB):
-            nc.sync.dma_start(x_sb[a][:], x[a * P:(a + 1) * P, :])
-            load_w(Q, 0, a)
-            load_w(K, 0, a)
+        def load_w(queue, part, c, first_block, count):
+            return load_blocks(queue, w_rows, part * D + c * CH, first_block, count, f"w{part}{c}")
 
+        x_sb = []
+        w_sb = [[[], []] for part in (Q, K, V)]
+        for a in range(0, KB, 2):
+            x_sb += load_blocks(nc.sync, x_rows, 0, a, 2, "x")
+            w_sb[Q][0] += load_w(nc.scalar, Q, 0, a, 2)
+            w_sb[K][0] += load_w(nc.sync, K, 0, a, 2)
         rb_sb = held.tile([P, NH], BF16, name="rb_sb")
         wb_sb = held.tile([P, NH], BF16, name="wb_sb")
         table = held.tile([P, T], F32, name="table")
-        mask_sb = [held.tile([P, T], F32, name=f"mask{ub}") for ub in range(TB)]
-        nc.sync.dma_start(rb_sb[:], rb)
-        nc.sync.dma_start(wb_sb[:], wb)
-        nc.sync.dma_start(table[:], r_emb)
-        for ub in range(TB):
-            nc.sync.dma_start(mask_sb[ub][:], mask[ub * P:(ub + 1) * P, :])
-        wfc_sb = [held.tile([P, D], BF16, name=f"wfc{h}") for h in range(NH)]
+        mask_sb = held.tile([P, TB, T], F32, name="mask_sb")
+        wfc_sb = held.tile([P, NH, D], BF16, name="wfc_sb")
+        nc.scalar.dma_start(rb_sb[:], rb)
+        nc.scalar.dma_start(wb_sb[:], wb)
+        nc.scalar.dma_start(table[:], r_emb)
+        nc.scalar.dma_start(mask_sb[:], mask.rearrange("(b p) t -> p b t", p=P))
+        w_sb[V][0] = load_w(nc.sync, V, 0, 0, KB)
+        w_sb[Q][1] = load_w(nc.scalar, Q, 1, 0, KB)
+        w_sb[K][1] = load_w(nc.sync, K, 1, 0, KB)
+        w_sb[V][1] = load_w(nc.scalar, V, 1, 0, KB)
+        nc.sync.dma_start(wfc_sb[:], w_fc.rearrange("(h p) m -> p h m", p=P))
 
         warm = held.tile([P, 1], F32, name="warm")
         nc.vector.memset(warm[:], 0.0)
@@ -76,33 +85,39 @@ def tile_relativemultiheadattention_b_kernel(tc, x, w_qkv, w_fc, rb, wb, r_emb, 
         val_t = [[held.tile([P, CH], BF16, name=f"val_t{c}{ub}") for ub in range(TB)]
                  for c in range(NH // HPC)]
         o_bf = [held.tile([P, T], BF16, name=f"o{h}") for h in range(NH)]
-        out_sb = [held.tile([P, T], F32, name=f"out_sb{m}") for m in range(D // P)]
+        out_sb = [held.tile([P, T], F32, name=f"out_sb{m}") for m in range(MB)]
         mask_t = [held.tile([P, T], F32, name=f"mask_t{tb}") for tb in range(TB)]
+
+        def group(pairs, finish):
+            bank = [None]
+            return [(bank, lhsT, rhs, i == 0, i == len(pairs) - 1, finish) for i, (lhsT, rhs) in enumerate(pairs)]
+
+        def issue(matmuls):
+            for bank, lhsT, rhs, first, last, finish in matmuls:
+                if first:
+                    bank[0] = banks.tile([P, T], F32, name="acc", tag="bank")
+                nc.tensor.matmul(bank[0][:], lhsT=lhsT, rhs=rhs, start=first, stop=last)
+                if last:
+                    finish(bank[0])
+
+        def copy_to(dest):
+            return lambda bank: nc.scalar.copy(dest[:], bank[:])
+
+        def add_to(dest):
+            return lambda bank: nc.vector.tensor_tensor(dest[:], bank[:], dest[:], ADD)
 
         def project_head(part, h):
             col = (h % HPC) * P
-            acc = banks.tile([P, T], F32, name="acc", tag="bank")
-            for a in range(KB):
-                nc.tensor.matmul(acc[:], lhsT=w_sb[part][h // HPC][a][:, col:col + P], rhs=x_sb[a][:],
-                                 start=(a == 0), stop=(a == KB - 1))
-            nc.scalar.copy(qk_bf[part][h][:], acc[:])
+            return group([(w_sb[part][h // HPC][a][:, col:col + P], x_sb[a]) for a in range(KB)],
+                         copy_to(qk_bf[part][h]))
 
         def project_values(c, ub):
-            acc = banks.tile([P, CH], F32, name="acc", tag="bank")
-            for a in range(KB):
-                nc.tensor.matmul(acc[:], lhsT=x_sb[a][:, ub * P:(ub + 1) * P], rhs=w_sb[V][c][a][:],
-                                 start=(a == 0), stop=(a == KB - 1))
-            nc.scalar.copy(val_t[c][ub][:], acc[:])
+            return group([(x_sb[a][:, ub * P:(ub + 1) * P], w_sb[V][c][a]) for a in range(KB)],
+                         copy_to(val_t[c][ub]))
 
         def project_output(m, heads):
-            acc = banks.tile([P, T], F32, name="acc", tag="bank")
-            for h in heads:
-                nc.tensor.matmul(acc[:], lhsT=wfc_sb[h][:, m * P:(m + 1) * P], rhs=o_bf[h][:],
-                                 start=(h == heads[0]), stop=(h == heads[-1]))
-            if heads[0] == 0:
-                nc.scalar.copy(out_sb[m][:], acc[:])
-            else:
-                nc.vector.tensor_tensor(out_sb[m][:], acc[:], out_sb[m][:], ADD)
+            return group([(wfc_sb[:, h, m * P:(m + 1) * P], o_bf[h][:]) for h in heads],
+                         copy_to(out_sb[m]) if heads[0] == 0 else add_to(out_sb[m]))
 
         sc = [[None, None] for h in range(NH)]
         a_bf = [None] * NH
@@ -110,10 +125,8 @@ def tile_relativemultiheadattention_b_kernel(tc, x, w_qkv, w_fc, rb, wb, r_emb, 
 
         def scalars(h):
             for part, wide in ((Q, rb_wide), (K, wb_wide)):
-                acc = banks.tile([P, T], F32, name="acc", tag="bank")
-                nc.tensor.matmul(acc[:], lhsT=wide[:, h, :], rhs=qk_bf[part][h][:], start=True, stop=True)
                 sc[h][part] = per_head.tile([P, T], F32, name=f"sc{part}", tag=f"sc{part}")
-                nc.scalar.copy(sc[h][part][:], acc[:])
+                issue(group([(wide[:, h, :], qk_bf[part][h][:])], copy_to(sc[h][part])))
 
         def look_up(h, part):
             first = part * (T // 16)
@@ -168,17 +181,14 @@ def tile_relativemultiheadattention_b_kernel(tc, x, w_qkv, w_fc, rb, wb, r_emb, 
 
         def meet_values(h):
             col = (h % HPC) * P
-            o_ps = banks.tile([P, T], F32, name="o_ps", tag="bank")
-            for ub in range(TB):
-                nc.tensor.matmul(o_ps[:], lhsT=val_t[h // HPC][ub][:, col:col + P], rhs=attn_t[h][:, ub, :],
-                                 start=(ub == 0), stop=(ub == TB - 1))
-            nc.scalar.copy(o_bf[h][:], o_ps[:])
+            issue(group([(val_t[h // HPC][ub][:, col:col + P], attn_t[h][:, ub, :]) for ub in range(TB)],
+                        copy_to(o_bf[h])))
 
         first_four = [(part, h) for h in (0, 1) for part in (Q, K)]
         accs = [banks.tile([P, T], F32, name=f"acc{part}{h}", tag="bank") for part, h in first_four]
         for a in range(KB):
             for acc, (part, h) in zip(accs, first_four):
-                nc.tensor.matmul(acc[:], lhsT=w_sb[part][0][a][:, h * P:(h + 1) * P], rhs=x_sb[a][:],
+                nc.tensor.matmul(acc[:], lhsT=w_sb[part][0][a][:, h * P:(h + 1) * P], rhs=x_sb[a],
                                  start=(a == 0), stop=(a == KB - 1))
         for acc, (part, h) in zip(accs, first_four):
             if part == Q:
@@ -186,41 +196,35 @@ def tile_relativemultiheadattention_b_kernel(tc, x, w_qkv, w_fc, rb, wb, r_emb, 
             else:
                 nc.vector.tensor_copy(qk_bf[part][h][:], acc[:])
 
-        ahead = [(project_head, (part, h)) for h in (2, 3) for part in (Q, K)]
-        ahead += [(project_values, (0, ub)) for ub in range(TB)]
-        ahead += [(project_head, (part, h)) for h in range(HPC, NH) for part in (Q, K)]
-        ahead += [(project_values, (1, ub)) for ub in range(TB)]
-
         scalars(0)
-        for a in range(KB):
-            load_w(V, 0, a)
-        project_head(*ahead[0][1])
+        issue(project_head(Q, 2))
         query_side(0)
         key_side(0)
         for tb in range(TB):
             flipped = banks.tile([P, T], F32, name="mask_flipped", tag="bank")
             for ub in range(TB):
-                nc.tensor.transpose(flipped[:, ub * P:(ub + 1) * P],
-                                    mask_sb[ub][:, tb * P:(tb + 1) * P], ident_f32[:])
+                nc.tensor.transpose(flipped[:, ub * P:(ub + 1) * P], mask_sb[:, ub, tb * P:(tb + 1) * P], ident_f32[:])
             nc.scalar.copy(mask_t[tb][:], flipped[:])
-        project_head(*ahead[1][1])
-        ahead = ahead[2:]
+        issue(project_head(K, 2))
 
-        first_output_step = TB * (HPC - 1) + VALUES_LAG + 1
         shares = [[0, 1, 2, 3], [4, 5], [6, 7]]
+        background = []
+        for ub in range(TB):
+            background += project_values(0, ub)
+        for h in (3, 4, 5, 6):
+            background += project_head(Q, h) + project_head(K, h)
+        for ub in range(TB):
+            background += project_values(1, ub)
+        background += project_head(Q, 7) + project_head(K, 7)
+        for m in range(MB):
+            background += project_output(m, shares[0])
+        rate = -(-len(background) // STEPS)
+        drain = []
+        for m in range(MB):
+            drain += project_output(m, shares[1])
 
         for n in range(STEPS + VALUES_LAG - TB + 1):
             h, tb = divmod(n, TB)
-            if n == 0:
-                for a in range(KB):
-                    load_w(Q, 1, a)
-                    load_w(K, 1, a)
-            if n == TB:
-                for a in range(KB):
-                    load_w(V, 1, a)
-                for g in range(NH):
-                    nc.scalar.dma_start(wfc_sb[g][:], w_fc[g * P:(g + 1) * P, :])
-
             if 1 <= n <= STEPS:
                 normalise(n - 1)
             if n < STEPS:
@@ -232,17 +236,15 @@ def tile_relativemultiheadattention_b_kernel(tc, x, w_qkv, w_fc, rb, wb, r_emb, 
                     query_side(h + 1)
                 if tb == 2:
                     key_side(h + 1)
-            if n < len(ahead):
-                work, args = ahead[n]
-                work(*args)
-            if n >= first_output_step:
-                share, m = divmod(n - first_output_step, D // P)
-                project_output(m, shares[share])
+            issue(background[n * rate:(n + 1) * rate])
+            if n >= STEPS:
+                issue(drain[(n - STEPS) * rate:(n - STEPS + 1) * rate])
             if 0 <= n - FLIP_LAG < STEPS:
                 flip(n - FLIP_LAG)
             if n >= VALUES_LAG and (n - VALUES_LAG) % TB == 0:
                 meet_values((n - VALUES_LAG) // TB)
 
-        for m in range(D // P):
-            project_output(m, shares[2])
-            nc.sync.dma_start(out[m * P:(m + 1) * P, :], out_sb[m][:])
+        for m in range(MB):
+            issue(project_output(m, shares[2]))
+            queue = nc.sync if m % 2 == 0 else nc.scalar
+            queue.dma_start(out[m * P:(m + 1) * P, :], out_sb[m][:])

@@ -18,7 +18,7 @@ HPC = CH // P
 NLIST = 1024
 Q, K, V = 0, 1, 2
 STEPS = NH * TB
-FLIP_LAG = 2
+FLIP_LAG = 3
 VALUES_LAG = TB + FLIP_LAG + 1
 
 FLOPS = 2 * D * 3 * D * T + 2 * P * NH * NLIST + 3 * 2 * NH * T * T * P + 2 * D * D * T
@@ -29,14 +29,11 @@ def tile_relativemultiheadattention_b_kernel(tc, x, w_qkv, w_fc, rb, wb, r_emb, 
     with (
         tc.tile_pool(name="held", bufs=1) as held,
         tc.tile_pool(name="per_head", bufs=2) as per_head,
-        tc.tile_pool(name="per_block", bufs=3) as per_block,
+        tc.tile_pool(name="per_block", bufs=4) as per_block,
         tc.tile_pool(name="stats", bufs=4) as stats,
         tc.psum_pool(name="banks", bufs=6) as banks,
         tc.psum_pool(name="flips", bufs=2) as flips,
     ):
-        offsets = held.tile([P, NLIST // 16], U16, name="offsets")
-        nc.sync.dma_start(offsets[:], offs)
-
         x_rows = x.rearrange("(a p) t -> p a t", p=P)
         w_rows = w_qkv.rearrange("(a p) r -> p a r", p=P)
 
@@ -54,6 +51,8 @@ def tile_relativemultiheadattention_b_kernel(tc, x, w_qkv, w_fc, rb, wb, r_emb, 
             x_sb += load_blocks(nc.sync, x_rows, 0, a, 2, "x")
             w_sb[Q][0] += load_w(nc.scalar, Q, 0, a, 2)
             w_sb[K][0] += load_w(nc.sync, K, 0, a, 2)
+        offsets = held.tile([P, NLIST // 16], U16, name="offsets")
+        nc.sync.dma_start(offsets[:], offs)
         rb_sb = held.tile([P, NH], BF16, name="rb_sb")
         wb_sb = held.tile([P, NH], BF16, name="wb_sb")
         table = held.tile([P, T], F32, name="table")
@@ -216,19 +215,19 @@ def tile_relativemultiheadattention_b_kernel(tc, x, w_qkv, w_fc, rb, wb, r_emb, 
         for ub in range(TB):
             background += project_values(1, ub)
         background += project_head(Q, 7) + project_head(K, 7)
-        for m in range(MB):
-            background += project_output(m, shares[0])
-        rate = -(-len(background) // STEPS)
+        rate = len(background) // (STEPS - MB)
         drain = []
         for m in range(MB):
             drain += project_output(m, shares[1])
 
         for n in range(STEPS + VALUES_LAG - TB + 1):
             h, tb = divmod(n, TB)
-            if 1 <= n <= STEPS:
-                normalise(n - 1)
+            if 0 <= n - FLIP_LAG < STEPS:
+                flip(n - FLIP_LAG)
             if n < STEPS:
                 scores_and_exp(n)
+            if 1 <= n <= STEPS:
+                normalise(n - 1)
             if h + 1 < NH:
                 if tb == 0:
                     scalars(h + 1)
@@ -237,10 +236,10 @@ def tile_relativemultiheadattention_b_kernel(tc, x, w_qkv, w_fc, rb, wb, r_emb, 
                 if tb == 2:
                     key_side(h + 1)
             issue(background[n * rate:(n + 1) * rate])
+            if STEPS - MB <= n < STEPS:
+                issue(project_output(n - (STEPS - MB), shares[0]))
             if n >= STEPS:
                 issue(drain[(n - STEPS) * rate:(n - STEPS + 1) * rate])
-            if 0 <= n - FLIP_LAG < STEPS:
-                flip(n - FLIP_LAG)
             if n >= VALUES_LAG and (n - VALUES_LAG) % TB == 0:
                 meet_values((n - VALUES_LAG) // TB)
 

@@ -15,11 +15,15 @@ MB = D // P
 TB = T // P
 CH = 512
 HPC = CH // P
-NLIST = 1024
+NLIST = 2 * T
+HALF = T // 16
 Q, K, V = 0, 1, 2
+
 STEPS = NH * TB
-FLIP_LAG = 3
-VALUES_LAG = TB + FLIP_LAG + 1
+EXP_LAG = 1
+SCALE_LAG = 2
+FLIP_LAG = 4
+VALUES_LAG = TB + FLIP_LAG
 
 FLOPS = 2 * D * 3 * D * T + 2 * P * NH * NLIST + 3 * 2 * NH * T * T * P + 2 * D * D * T
 
@@ -29,8 +33,8 @@ def tile_relativemultiheadattention_b_kernel(tc, x, w_qkv, w_fc, rb, wb, r_emb, 
     with (
         tc.tile_pool(name="held", bufs=1) as held,
         tc.tile_pool(name="per_head", bufs=2) as per_head,
-        tc.tile_pool(name="per_block", bufs=4) as per_block,
-        tc.tile_pool(name="stats", bufs=4) as stats,
+        tc.tile_pool(name="per_block", bufs=FLIP_LAG) as per_block,
+        tc.tile_pool(name="stats", bufs=FLIP_LAG) as stats,
         tc.psum_pool(name="banks", bufs=6) as banks,
         tc.psum_pool(name="flips", bufs=2) as flips,
     ):
@@ -81,8 +85,7 @@ def tile_relativemultiheadattention_b_kernel(tc, x, w_qkv, w_fc, rb, wb, r_emb, 
         nc.vector.tensor_copy(wb_wide[:], wb_sb[:].unsqueeze(2).to_broadcast([P, NH, P]))
 
         qk_bf = [[held.tile([P, T], BF16, name=f"qk{part}{h}") for h in range(NH)] for part in (Q, K)]
-        val_t = [[held.tile([P, CH], BF16, name=f"val_t{c}{ub}") for ub in range(TB)]
-                 for c in range(NH // HPC)]
+        val_t = [[held.tile([P, CH], BF16, name=f"val_t{c}{ub}") for ub in range(TB)] for c in range(NH // HPC)]
         o_bf = [held.tile([P, T], BF16, name=f"o{h}") for h in range(NH)]
         out_sb = [held.tile([P, T], F32, name=f"out_sb{m}") for m in range(MB)]
         mask_t = [held.tile([P, T], F32, name=f"mask_t{tb}") for tb in range(TB)]
@@ -94,7 +97,7 @@ def tile_relativemultiheadattention_b_kernel(tc, x, w_qkv, w_fc, rb, wb, r_emb, 
         def issue(matmuls):
             for bank, lhsT, rhs, first, last, finish in matmuls:
                 if first:
-                    bank[0] = banks.tile([P, T], F32, name="acc", tag="bank")
+                    bank[0] = banks.tile([P, T], F32, name="bank", tag="bank")
                 nc.tensor.matmul(bank[0][:], lhsT=lhsT, rhs=rhs, start=first, stop=last)
                 if last:
                     finish(bank[0])
@@ -105,16 +108,16 @@ def tile_relativemultiheadattention_b_kernel(tc, x, w_qkv, w_fc, rb, wb, r_emb, 
         def add_to(dest):
             return lambda bank: nc.vector.tensor_tensor(dest[:], bank[:], dest[:], ADD)
 
-        def project_head(part, h):
+        def head_projection(part, h):
             col = (h % HPC) * P
             return group([(w_sb[part][h // HPC][a][:, col:col + P], x_sb[a]) for a in range(KB)],
                          copy_to(qk_bf[part][h]))
 
-        def project_values(c, ub):
+        def values_projection(c, ub):
             return group([(x_sb[a][:, ub * P:(ub + 1) * P], w_sb[V][c][a]) for a in range(KB)],
                          copy_to(val_t[c][ub]))
 
-        def project_output(m, heads):
+        def output_share(m, heads):
             return group([(wfc_sb[:, h, m * P:(m + 1) * P], o_bf[h][:]) for h in heads],
                          copy_to(out_sb[m]) if heads[0] == 0 else add_to(out_sb[m]))
 
@@ -128,9 +131,8 @@ def tile_relativemultiheadattention_b_kernel(tc, x, w_qkv, w_fc, rb, wb, r_emb, 
                 issue(group([(wide[:, h, :], qk_bf[part][h][:])], copy_to(sc[h][part])))
 
         def look_up(h, part):
-            first = part * (T // 16)
             rel = per_head.tile([P, T], F32, name=f"rel{part}", tag=f"rel{part}")
-            picked = table[:].indirect(offsets[:, first:first + T // 16])
+            picked = table[:].indirect(offsets[:, part * HALF:(part + 1) * HALF])
             nc.vector.tensor_tensor(rel[:], picked, sc[h][part][:], MULT)
             return rel
 
@@ -144,26 +146,28 @@ def tile_relativemultiheadattention_b_kernel(tc, x, w_qkv, w_fc, rb, wb, r_emb, 
             kr_bf[h] = per_head.tile([P, T], BF16, name="kr_bf", tag="kr_bf")
             nc.vector.tensor_copy(kr_bf[h][:], rel[:])
 
+        scores = [None] * STEPS
+        neg_max = [None] * STEPS
         expd = [None] * STEPS
         row_sum = [None] * STEPS
         attn = [None] * STEPS
         attn_t = [None] * NH
 
-        def scores_and_exp(n):
+        def scores_and_max(n):
             h, tb = divmod(n, TB)
             block = slice(tb * P, (tb + 1) * P)
-            scores_ps = banks.tile([P, T], F32, name="scores_ps", tag="bank")
-            nc.tensor.matmul(scores_ps[:], lhsT=a_bf[h][:, block], rhs=qk_bf[K][h][:], start=True, stop=False)
-            nc.tensor.matmul(scores_ps[:], lhsT=qk_bf[Q][h][:, block], rhs=kr_bf[h][:], start=False, stop=True)
-            scores = per_block.tile([P, T], F32, name="scores", tag="scores")
-            nc.vector.tensor_tensor(scores[:], scores_ps[:], mask_t[tb][:], ADD)
-            neg_max = stats.tile([P, 1], F32, name="neg_max", tag="neg_max")
-            nc.vector.tensor_reduce(neg_max[:], scores[:], AXIS_X, MAX, negate=True)
+            scores[n] = per_block.tile([P, T], F32, name="scores", tag="scores")
+            with_mask = lambda bank: nc.vector.tensor_tensor(scores[n][:], bank[:], mask_t[tb][:], ADD)
+            issue(group([(a_bf[h][:, block], qk_bf[K][h][:]), (qk_bf[Q][h][:, block], kr_bf[h][:])], with_mask))
+            neg_max[n] = stats.tile([P, 1], F32, name="neg_max", tag="neg_max")
+            nc.vector.tensor_reduce(neg_max[n][:], scores[n][:], AXIS_X, MAX, negate=True)
+
+        def exponentials(n):
             expd[n] = per_block.tile([P, T], F32, name="expd", tag="expd")
             row_sum[n] = stats.tile([P, 1], F32, name="row_sum", tag="row_sum")
-            nc.scalar.activation(expd[n][:], scores[:], EXP, bias=neg_max[:], scale=1.0, accum_out=row_sum[n][:])
+            nc.scalar.activation(expd[n][:], scores[n][:], EXP, bias=neg_max[n][:], scale=1.0, accum_out=row_sum[n][:])
 
-        def normalise(n):
+        def scale(n):
             inv_sum = stats.tile([P, 1], F32, name="inv_sum", tag="inv_sum")
             nc.vector.reciprocal(inv_sum[:], row_sum[n][:])
             attn[n] = per_block.tile([P, T], BF16, name="attn", tag="attn")
@@ -184,50 +188,52 @@ def tile_relativemultiheadattention_b_kernel(tc, x, w_qkv, w_fc, rb, wb, r_emb, 
                         copy_to(o_bf[h])))
 
         first_four = [(part, h) for h in (0, 1) for part in (Q, K)]
-        accs = [banks.tile([P, T], F32, name=f"acc{part}{h}", tag="bank") for part, h in first_four]
+        four_banks = [banks.tile([P, T], F32, name=f"bank{part}{h}", tag="bank") for part, h in first_four]
         for a in range(KB):
-            for acc, (part, h) in zip(accs, first_four):
-                nc.tensor.matmul(acc[:], lhsT=w_sb[part][0][a][:, h * P:(h + 1) * P], rhs=x_sb[a],
+            for bank, (part, h) in zip(four_banks, first_four):
+                nc.tensor.matmul(bank[:], lhsT=w_sb[part][0][a][:, h * P:(h + 1) * P], rhs=x_sb[a],
                                  start=(a == 0), stop=(a == KB - 1))
-        for acc, (part, h) in zip(accs, first_four):
+        for bank, (part, h) in zip(four_banks, first_four):
             if part == Q:
-                nc.scalar.copy(qk_bf[part][h][:], acc[:])
+                nc.scalar.copy(qk_bf[part][h][:], bank[:])
             else:
-                nc.vector.tensor_copy(qk_bf[part][h][:], acc[:])
+                nc.vector.tensor_copy(qk_bf[part][h][:], bank[:])
 
         scalars(0)
-        issue(project_head(Q, 2))
+        issue(head_projection(Q, 2))
         query_side(0)
         key_side(0)
         for tb in range(TB):
-            flipped = banks.tile([P, T], F32, name="mask_flipped", tag="bank")
+            mask_flipped = banks.tile([P, T], F32, name="mask_flipped", tag="bank")
             for ub in range(TB):
-                nc.tensor.transpose(flipped[:, ub * P:(ub + 1) * P], mask_sb[:, ub, tb * P:(tb + 1) * P], ident_f32[:])
-            nc.scalar.copy(mask_t[tb][:], flipped[:])
-        issue(project_head(K, 2))
+                nc.tensor.transpose(mask_flipped[:, ub * P:(ub + 1) * P], mask_sb[:, ub, tb * P:(tb + 1) * P], ident_f32[:])
+            nc.scalar.copy(mask_t[tb][:], mask_flipped[:])
+        issue(head_projection(K, 2))
 
-        shares = [[0, 1, 2, 3], [4, 5], [6, 7]]
         background = []
         for ub in range(TB):
-            background += project_values(0, ub)
-        for h in (3, 4, 5, 6):
-            background += project_head(Q, h) + project_head(K, h)
+            background += values_projection(0, ub)
+        for h in range(3, NH):
+            background += head_projection(Q, h) + head_projection(K, h)
         for ub in range(TB):
-            background += project_values(1, ub)
-        background += project_head(Q, 7) + project_head(K, 7)
+            background += values_projection(1, ub)
         rate = len(background) // (STEPS - MB)
-        drain = []
+        shares = [[0, 1, 2, 3], [4, 5], [6, 7]]
+        second_share = []
         for m in range(MB):
-            drain += project_output(m, shares[1])
+            second_share += output_share(m, shares[1])
+        late_rate = len(second_share) // FLIP_LAG
 
         for n in range(STEPS + VALUES_LAG - TB + 1):
             h, tb = divmod(n, TB)
             if 0 <= n - FLIP_LAG < STEPS:
                 flip(n - FLIP_LAG)
+            if 0 <= n - EXP_LAG < STEPS:
+                exponentials(n - EXP_LAG)
             if n < STEPS:
-                scores_and_exp(n)
-            if 1 <= n <= STEPS:
-                normalise(n - 1)
+                scores_and_max(n)
+            if 0 <= n - SCALE_LAG < STEPS:
+                scale(n - SCALE_LAG)
             if h + 1 < NH:
                 if tb == 0:
                     scalars(h + 1)
@@ -237,13 +243,13 @@ def tile_relativemultiheadattention_b_kernel(tc, x, w_qkv, w_fc, rb, wb, r_emb, 
                     key_side(h + 1)
             issue(background[n * rate:(n + 1) * rate])
             if STEPS - MB <= n < STEPS:
-                issue(project_output(n - (STEPS - MB), shares[0]))
+                issue(output_share(n - (STEPS - MB), shares[0]))
             if n >= STEPS:
-                issue(drain[(n - STEPS) * rate:(n - STEPS + 1) * rate])
+                issue(second_share[(n - STEPS) * late_rate:(n - STEPS + 1) * late_rate])
             if n >= VALUES_LAG and (n - VALUES_LAG) % TB == 0:
                 meet_values((n - VALUES_LAG) // TB)
 
         for m in range(MB):
-            issue(project_output(m, shares[2]))
+            issue(output_share(m, shares[2]))
             queue = nc.sync if m % 2 == 0 else nc.scalar
             queue.dma_start(out[m * P:(m + 1) * P, :], out_sb[m][:])

@@ -173,13 +173,14 @@ def tile_relativemultiheadattention_b_kernel(tc, x, w_qkv, w_fc, rb, wb, r_emb, 
             attn[n] = per_block.tile([P, T], BF16, name="attn", tag="attn")
             nc.gpsimd.tensor_scalar(attn[n][:], expd[n][:], inv_sum[:], 0.0, MULT, ADD)
 
-        def flip(n):
+        def flip(n, between):
             h, tb = divmod(n, TB)
             if tb == 0:
                 attn_t[h] = per_head.tile([P, TB, T], BF16, name="attn_t", tag="attn_t")
             flipped = flips.tile([P, TB, P], BF16, name="flipped", tag="flipped")
             for ub in range(TB):
                 nc.tensor.transpose(flipped[:, ub, :], attn[n][:, ub * P:(ub + 1) * P], ident_bf[:])
+                issue(between[ub])
             nc.scalar.copy(attn_t[h][:, :, tb * P:(tb + 1) * P], flipped[:])
 
         def meet_values(h):
@@ -226,8 +227,6 @@ def tile_relativemultiheadattention_b_kernel(tc, x, w_qkv, w_fc, rb, wb, r_emb, 
 
         for n in range(STEPS + VALUES_LAG - TB + 1):
             h, tb = divmod(n, TB)
-            if 0 <= n - FLIP_LAG < STEPS:
-                flip(n - FLIP_LAG)
             if 0 <= n - EXP_LAG < STEPS:
                 exponentials(n - EXP_LAG)
             if n < STEPS:
@@ -241,11 +240,15 @@ def tile_relativemultiheadattention_b_kernel(tc, x, w_qkv, w_fc, rb, wb, r_emb, 
                     query_side(h + 1)
                 if tb == 2:
                     key_side(h + 1)
-            issue(background[n * rate:(n + 1) * rate])
+            filler = background[n * rate:(n + 1) * rate]
             if STEPS - MB <= n < STEPS:
-                issue(output_share(n - (STEPS - MB), shares[0]))
+                filler = filler + output_share(n - (STEPS - MB), shares[0])
             if n >= STEPS:
-                issue(second_share[(n - STEPS) * late_rate:(n - STEPS + 1) * late_rate])
+                filler = filler + second_share[(n - STEPS) * late_rate:(n - STEPS + 1) * late_rate]
+            if 0 <= n - FLIP_LAG < STEPS:
+                flip(n - FLIP_LAG, [filler[ub * len(filler) // TB:(ub + 1) * len(filler) // TB] for ub in range(TB)])
+            else:
+                issue(filler)
             if n >= VALUES_LAG and (n - VALUES_LAG) % TB == 0:
                 meet_values((n - VALUES_LAG) // TB)
 

@@ -211,10 +211,10 @@ def tile_relativemultiheadattention_b_kernel(tc, x, w_qkv, w_fc, rb, wb, r_emb, 
             nc.scalar.copy(mask_t[tb][:], mask_flipped[:])
         issue(head_projection(K, 2))
 
-        background = []
+        background = head_projection(Q, 3) + head_projection(K, 3)
         for ub in range(TB):
             background += values_projection(0, ub)
-        for h in range(3, NH):
+        for h in range(4, NH):
             background += head_projection(Q, h) + head_projection(K, h)
         for ub in range(TB):
             background += values_projection(1, ub)
@@ -225,7 +225,7 @@ def tile_relativemultiheadattention_b_kernel(tc, x, w_qkv, w_fc, rb, wb, r_emb, 
             second_share += output_share(m, shares[1])
         late_rate = len(second_share) // FLIP_LAG
 
-        for n in range(STEPS + VALUES_LAG - TB + 1):
+        for n in range(STEPS + FLIP_LAG):
             h, tb = divmod(n, TB)
             if 0 <= n - EXP_LAG < STEPS:
                 exponentials(n - EXP_LAG)
@@ -252,7 +252,16 @@ def tile_relativemultiheadattention_b_kernel(tc, x, w_qkv, w_fc, rb, wb, r_emb, 
             if n >= VALUES_LAG and (n - VALUES_LAG) % TB == 0:
                 meet_values((n - VALUES_LAG) // TB)
 
+        OPEN_EARLY, OPEN_AHEAD = 2, 5
+        last_share = [output_share(m, shares[2]) for m in range(MB)]
+        for m in range(OPEN_EARLY):
+            issue(last_share[m][:1])
+        meet_values(NH - 1)
+        for m in range(OPEN_EARLY, OPEN_AHEAD):
+            issue(last_share[m][:1])
         for m in range(MB):
-            issue(output_share(m, shares[2]))
+            issue(last_share[m][1:])
             queue = nc.sync if m % 2 == 0 else nc.scalar
             queue.dma_start(out[m * P:(m + 1) * P, :], out_sb[m][:])
+            if m + OPEN_AHEAD < MB:
+                issue(last_share[m + OPEN_AHEAD][:1])

@@ -139,7 +139,7 @@ def tile_relativemultiheadattention_b_kernel(tc, x, w_qkv, w_fc, rb, wb, r_emb, 
         def query_side(h):
             rel = look_up(h, Q)
             a_bf[h] = per_head.tile([P, T], BF16, name="a_bf", tag="a_bf")
-            nc.gpsimd.tensor_tensor(a_bf[h][:], rel[:], qk_bf[Q][h][:], ADD)
+            nc.vector.tensor_tensor(a_bf[h][:], rel[:], qk_bf[Q][h][:], ADD)
 
         def key_side(h):
             rel = look_up(h, K)
@@ -163,7 +163,7 @@ def tile_relativemultiheadattention_b_kernel(tc, x, w_qkv, w_fc, rb, wb, r_emb, 
             nc.vector.tensor_reduce(neg_max[n][:], scores[n][:], AXIS_X, MAX, negate=True)
 
         def exponentials(n):
-            expd[n] = per_block.tile([P, T], F32, name="expd", tag="expd")
+            expd[n] = per_block.tile([P, T], BF16, name="expd", tag="expd")
             row_sum[n] = stats.tile([P, 1], F32, name="row_sum", tag="row_sum")
             nc.scalar.activation(expd[n][:], scores[n][:], EXP, bias=neg_max[n][:], scale=1.0, accum_out=row_sum[n][:])
 
@@ -171,7 +171,7 @@ def tile_relativemultiheadattention_b_kernel(tc, x, w_qkv, w_fc, rb, wb, r_emb, 
             inv_sum = stats.tile([P, 1], F32, name="inv_sum", tag="inv_sum")
             nc.vector.reciprocal(inv_sum[:], row_sum[n][:])
             attn[n] = per_block.tile([P, T], BF16, name="attn", tag="attn")
-            nc.gpsimd.tensor_scalar(attn[n][:], expd[n][:], inv_sum[:], 0.0, MULT, ADD)
+            nc.vector.tensor_scalar(attn[n][:], expd[n][:], inv_sum[:], None, MULT)
 
         def flip(n, between):
             h, tb = divmod(n, TB)

@@ -35,8 +35,7 @@ def tile_relativemultiheadattention_b_kernel(tc, x, w_qkv, w_fc, rb, wb, r_emb, 
         tc.tile_pool(name="per_head", bufs=2) as per_head,
         tc.tile_pool(name="per_block", bufs=FLIP_LAG) as per_block,
         tc.tile_pool(name="stats", bufs=FLIP_LAG) as stats,
-        tc.psum_pool(name="banks", bufs=6) as banks,
-        tc.psum_pool(name="flips", bufs=2) as flips,
+        tc.psum_pool(name="banks", bufs=8) as banks,
     ):
         x_rows = x.rearrange("(a p) t -> p a t", p=P)
         w_rows = w_qkv.rearrange("(a p) r -> p a r", p=P)
@@ -177,7 +176,7 @@ def tile_relativemultiheadattention_b_kernel(tc, x, w_qkv, w_fc, rb, wb, r_emb, 
             h, tb = divmod(n, TB)
             if tb == 0:
                 attn_t[h] = per_head.tile([P, TB, T], BF16, name="attn_t", tag="attn_t")
-            flipped = flips.tile([P, TB, P], BF16, name="flipped", tag="flipped")
+            flipped = banks.tile([P, TB, P], BF16, name="flipped", tag="bank")
             for ub in range(TB):
                 nc.tensor.transpose(flipped[:, ub, :], attn[n][:, ub * P:(ub + 1) * P], ident_bf[:])
                 issue(between[ub])
@@ -220,8 +219,9 @@ def tile_relativemultiheadattention_b_kernel(tc, x, w_qkv, w_fc, rb, wb, r_emb, 
             background += values_projection(1, ub)
         rate = len(background) // (STEPS - MB)
         shares = [[0, 1, 2, 3], [4, 5], [6, 7]]
+        MERGED = 2
         second_share = []
-        for m in range(MB):
+        for m in range(MB - MERGED):
             second_share += output_share(m, shares[1])
         late_rate = len(second_share) // FLIP_LAG
 
@@ -252,16 +252,18 @@ def tile_relativemultiheadattention_b_kernel(tc, x, w_qkv, w_fc, rb, wb, r_emb, 
             if n >= VALUES_LAG and (n - VALUES_LAG) % TB == 0:
                 meet_values((n - VALUES_LAG) // TB)
 
-        OPEN_EARLY, OPEN_AHEAD = 2, 5
-        last_share = [output_share(m, shares[2]) for m in range(MB)]
+        OPEN_EARLY = 2
+        last_share = [output_share(m, shares[2] if m < MB - MERGED else shares[1] + shares[2]) for m in range(MB)]
         for m in range(OPEN_EARLY):
-            issue(last_share[m][:1])
+            issue(last_share[m][:-1])
         meet_values(NH - 1)
-        for m in range(OPEN_EARLY, OPEN_AHEAD):
-            issue(last_share[m][:1])
+        for m in range(OPEN_EARLY, MB - MERGED):
+            issue(last_share[m][:-1])
+        waiting = []
+        for m in range(MB - MERGED, MB):
+            waiting += last_share[m][:-1]
         for m in range(MB):
-            issue(last_share[m][1:])
+            issue(last_share[m][-1:])
             queue = nc.sync if m % 2 == 0 else nc.scalar
             queue.dma_start(out[m * P:(m + 1) * P, :], out_sb[m][:])
-            if m + OPEN_AHEAD < MB:
-                issue(last_share[m + OPEN_AHEAD][:1])
+            issue(waiting[m:m + 1])

@@ -219,11 +219,10 @@ def tile_relativemultiheadattention_b_kernel(tc, x, w_qkv, w_fc, rb, wb, r_emb, 
             background += values_projection(1, ub)
         rate = len(background) // (STEPS - MB)
         shares = [[0, 1, 2, 3], [4, 5], [6, 7]]
-        MERGED = 2
+        MERGED = 3
         second_share = []
         for m in range(MB - MERGED):
             second_share += output_share(m, shares[1])
-        late_rate = len(second_share) // FLIP_LAG
 
         for n in range(STEPS + FLIP_LAG):
             h, tb = divmod(n, TB)
@@ -244,7 +243,7 @@ def tile_relativemultiheadattention_b_kernel(tc, x, w_qkv, w_fc, rb, wb, r_emb, 
             if STEPS - MB <= n < STEPS:
                 filler = filler + output_share(n - (STEPS - MB), shares[0])
             if n >= STEPS:
-                filler = filler + second_share[(n - STEPS) * late_rate:(n - STEPS + 1) * late_rate]
+                filler = filler + second_share[(n - STEPS) * len(second_share) // FLIP_LAG:(n - STEPS + 1) * len(second_share) // FLIP_LAG]
             if 0 <= n - FLIP_LAG < STEPS:
                 flip(n - FLIP_LAG, [filler[ub * len(filler) // TB:(ub + 1) * len(filler) // TB] for ub in range(TB)])
             else:
@@ -266,4 +265,4 @@ def tile_relativemultiheadattention_b_kernel(tc, x, w_qkv, w_fc, rb, wb, r_emb, 
             issue(last_share[m][-1:])
             queue = nc.sync if m % 2 == 0 else nc.scalar
             queue.dma_start(out[m * P:(m + 1) * P, :], out_sb[m][:])
-            issue(waiting[m:m + 1])
+            issue(waiting[m * len(waiting) // (MB - 1):(m + 1) * len(waiting) // (MB - 1)])

import concourse.mybir as mybir
from concourse.masks import make_identity

BF16, F32, U16 = mybir.dt.bfloat16, mybir.dt.float32, mybir.dt.uint16
ADD, MULT, MAX = mybir.AluOpType.add, mybir.AluOpType.mult, mybir.AluOpType.max
EXP = mybir.ActivationFunctionType.Exp
AXIS_X = mybir.AxisListType.X

P = 128
D = 1024
T = 512
NH = 8
KB = D // P
MB = D // P
TB = T // P
CH = 512
HPC = CH // P
NLIST = 2 * T
HALF = T // 16
Q, K, V = 0, 1, 2

STEPS = NH * TB
EXP_LAG = 1
SCALE_LAG = 2
FLIP_LAG = 4
VALUES_LAG = TB + FLIP_LAG

FLOPS = 2 * D * 3 * D * T + 2 * P * NH * NLIST + 3 * 2 * NH * T * T * P + 2 * D * D * T


def tile_relativemultiheadattention_b_kernel(tc, x, w_qkv, w_fc, rb, wb, r_emb, mask, offs, out):
    nc = tc.nc
    with (
        tc.tile_pool(name="held", bufs=1) as held,
        tc.tile_pool(name="per_head", bufs=2) as per_head,
        tc.tile_pool(name="per_block", bufs=FLIP_LAG) as per_block,
        tc.tile_pool(name="stats", bufs=FLIP_LAG) as stats,
        tc.psum_pool(name="banks", bufs=8) as banks,
    ):
        x_rows = x.rearrange("(a p) t -> p a t", p=P)
        w_rows = w_qkv.rearrange("(a p) r -> p a r", p=P)

        def load_blocks(queue, rows, first_col, first_block, count, name):
            piece = held.tile([P, count, CH], BF16, name=f"{name}_{first_block}")
            queue.dma_start(piece[:], rows[:, first_block:first_block + count, first_col:first_col + CH])
            return [piece[:, i, :] for i in range(count)]

        def load_w(queue, part, c, first_block, count):
            return load_blocks(queue, w_rows, part * D + c * CH, first_block, count, f"w{part}{c}")

        x_sb = []
        w_sb = [[[], []] for part in (Q, K, V)]
        for a in range(0, KB, 2):
            x_sb += load_blocks(nc.sync, x_rows, 0, a, 2, "x")
            w_sb[Q][0] += load_w(nc.scalar, Q, 0, a, 2)
            w_sb[K][0] += load_w(nc.sync, K, 0, a, 2)
        offsets = held.tile([P, NLIST // 16], U16, name="offsets")
        nc.sync.dma_start(offsets[:], offs)
        rb_sb = held.tile([P, NH], BF16, name="rb_sb")
        wb_sb = held.tile([P, NH], BF16, name="wb_sb")
        table = held.tile([P, T], F32, name="table")
        mask_sb = held.tile([P, TB, T], F32, name="mask_sb")
        wfc_sb = held.tile([P, NH, D], BF16, name="wfc_sb")
        nc.scalar.dma_start(rb_sb[:], rb)
        nc.scalar.dma_start(wb_sb[:], wb)
        nc.scalar.dma_start(table[:], r_emb)
        nc.scalar.dma_start(mask_sb[:], mask.rearrange("(b p) t -> p b t", p=P))
        w_sb[V][0] = load_w(nc.sync, V, 0, 0, KB)
        w_sb[Q][1] = load_w(nc.scalar, Q, 1, 0, KB)
        w_sb[K][1] = load_w(nc.sync, K, 1, 0, KB)
        w_sb[V][1] = load_w(nc.scalar, V, 1, 0, KB)
        nc.sync.dma_start(wfc_sb[:], w_fc.rearrange("(h p) m -> p h m", p=P))

        warm = held.tile([P, 1], F32, name="warm")
        nc.vector.memset(warm[:], 0.0)
        nc.scalar.activation(warm[:], warm[:], EXP)
        ident_f32 = held.tile([P, P], F32, name="ident_f32")
        ident_bf = held.tile([P, P], BF16, name="ident_bf")
        make_identity(nc, ident_f32[:])
        make_identity(nc, ident_bf[:])
        rb_wide = held.tile([P, NH, P], BF16, name="rb_wide")
        wb_wide = held.tile([P, NH, P], BF16, name="wb_wide")
        nc.vector.tensor_copy(rb_wide[:], rb_sb[:].unsqueeze(2).to_broadcast([P, NH, P]))
        nc.vector.tensor_copy(wb_wide[:], wb_sb[:].unsqueeze(2).to_broadcast([P, NH, P]))

        qk_bf = [[held.tile([P, T], BF16, name=f"qk{part}{h}") for h in range(NH)] for part in (Q, K)]
        val_t = [[held.tile([P, CH], BF16, name=f"val_t{c}{ub}") for ub in range(TB)] for c in range(NH // HPC)]
        o_bf = [held.tile([P, T], BF16, name=f"o{h}") for h in range(NH)]
        out_sb = [held.tile([P, T], F32, name=f"out_sb{m}") for m in range(MB)]
        mask_t = [held.tile([P, T], F32, name=f"mask_t{tb}") for tb in range(TB)]

        def group(pairs, finish):
            bank = [None]
            return [(bank, lhsT, rhs, i == 0, i == len(pairs) - 1, finish) for i, (lhsT, rhs) in enumerate(pairs)]

        def issue(matmuls):
            for bank, lhsT, rhs, first, last, finish in matmuls:
                if first:
                    bank[0] = banks.tile([P, T], F32, name="bank", tag="bank")
                nc.tensor.matmul(bank[0][:], lhsT=lhsT, rhs=rhs, start=first, stop=last)
                if last:
                    finish(bank[0])

        def copy_to(dest):
            return lambda bank: nc.scalar.copy(dest[:], bank[:])

        def add_to(dest):
            return lambda bank: nc.vector.tensor_tensor(dest[:], bank[:], dest[:], ADD)

        def head_projection(part, h):
            col = (h % HPC) * P
            return group([(w_sb[part][h // HPC][a][:, col:col + P], x_sb[a]) for a in range(KB)],
                         copy_to(qk_bf[part][h]))

        def values_projection(c, ub):
            return group([(x_sb[a][:, ub * P:(ub + 1) * P], w_sb[V][c][a]) for a in range(KB)],
                         copy_to(val_t[c][ub]))

        def output_share(m, heads):
            return group([(wfc_sb[:, h, m * P:(m + 1) * P], o_bf[h][:]) for h in heads],
                         copy_to(out_sb[m]) if heads[0] == 0 else add_to(out_sb[m]))

        sc = [[None, None] for h in range(NH)]
        a_bf = [None] * NH
        kr_bf = [None] * NH

        def scalars(h):
            for part, wide in ((Q, rb_wide), (K, wb_wide)):
                sc[h][part] = per_head.tile([P, T], F32, name=f"sc{part}", tag=f"sc{part}")
                issue(group([(wide[:, h, :], qk_bf[part][h][:])], copy_to(sc[h][part])))

        def look_up(h, part):
            rel = per_head.tile([P, T], F32, name=f"rel{part}", tag=f"rel{part}")
            picked = table[:].indirect(offsets[:, part * HALF:(part + 1) * HALF])
            nc.vector.tensor_tensor(rel[:], picked, sc[h][part][:], MULT)
            return rel

        def query_side(h):
            rel = look_up(h, Q)
            a_bf[h] = per_head.tile([P, T], BF16, name="a_bf", tag="a_bf")
            nc.vector.tensor_tensor(a_bf[h][:], rel[:], qk_bf[Q][h][:], ADD)

        def key_side(h):
            rel = look_up(h, K)
            kr_bf[h] = per_head.tile([P, T], BF16, name="kr_bf", tag="kr_bf")
            nc.vector.tensor_copy(kr_bf[h][:], rel[:])

        scores = [None] * STEPS
        neg_max = [None] * STEPS
        expd = [None] * STEPS
        row_sum = [None] * STEPS
        attn = [None] * STEPS
        attn_t = [None] * NH

        def scores_and_max(n):
            h, tb = divmod(n, TB)
            block = slice(tb * P, (tb + 1) * P)
            scores[n] = per_block.tile([P, T], F32, name="scores", tag="scores")
            with_mask = lambda bank: nc.vector.tensor_tensor(scores[n][:], bank[:], mask_t[tb][:], ADD)
            issue(group([(a_bf[h][:, block], qk_bf[K][h][:]), (qk_bf[Q][h][:, block], kr_bf[h][:])], with_mask))
            neg_max[n] = stats.tile([P, 1], F32, name="neg_max", tag="neg_max")
            nc.vector.tensor_reduce(neg_max[n][:], scores[n][:], AXIS_X, MAX, negate=True)

        def exponentials(n):
            expd[n] = per_block.tile([P, T], BF16, name="expd", tag="expd")
            row_sum[n] = stats.tile([P, 1], F32, name="row_sum", tag="row_sum")
            nc.scalar.activation(expd[n][:], scores[n][:], EXP, bias=neg_max[n][:], scale=1.0, accum_out=row_sum[n][:])

        def scale(n):
            inv_sum = stats.tile([P, 1], F32, name="inv_sum", tag="inv_sum")
            nc.vector.reciprocal(inv_sum[:], row_sum[n][:])
            attn[n] = per_block.tile([P, T], BF16, name="attn", tag="attn")
            nc.vector.tensor_scalar(attn[n][:], expd[n][:], inv_sum[:], None, MULT)

        def flip(n, between):
            h, tb = divmod(n, TB)
            if tb == 0:
                attn_t[h] = per_head.tile([P, TB, T], BF16, name="attn_t", tag="attn_t")
            flipped = banks.tile([P, TB, P], BF16, name="flipped", tag="bank")
            for ub in range(TB):
                nc.tensor.transpose(flipped[:, ub, :], attn[n][:, ub * P:(ub + 1) * P], ident_bf[:])
                issue(between[ub])
            nc.scalar.copy(attn_t[h][:, :, tb * P:(tb + 1) * P], flipped[:])

        def meet_values(h):
            col = (h % HPC) * P
            issue(group([(val_t[h // HPC][ub][:, col:col + P], attn_t[h][:, ub, :]) for ub in range(TB)],
                        copy_to(o_bf[h])))

        first_four = [(part, h) for h in (0, 1) for part in (Q, K)]
        four_banks = [banks.tile([P, T], F32, name=f"bank{part}{h}", tag="bank") for part, h in first_four]
        for a in range(KB):
            for bank, (part, h) in zip(four_banks, first_four):
                nc.tensor.matmul(bank[:], lhsT=w_sb[part][0][a][:, h * P:(h + 1) * P], rhs=x_sb[a],
                                 start=(a == 0), stop=(a == KB - 1))
        for bank, (part, h) in zip(four_banks, first_four):
            if part == Q:
                nc.scalar.copy(qk_bf[part][h][:], bank[:])
            else:
                nc.vector.tensor_copy(qk_bf[part][h][:], bank[:])

        scalars(0)
        issue(head_projection(Q, 2))
        query_side(0)
        key_side(0)
        for tb in range(TB):
            mask_flipped = banks.tile([P, T], F32, name="mask_flipped", tag="bank")
            for ub in range(TB):
                nc.tensor.transpose(mask_flipped[:, ub * P:(ub + 1) * P], mask_sb[:, ub, tb * P:(tb + 1) * P], ident_f32[:])
            nc.scalar.copy(mask_t[tb][:], mask_flipped[:])
        issue(head_projection(K, 2))

        background = head_projection(Q, 3) + head_projection(K, 3)
        for ub in range(TB):
            background += values_projection(0, ub)
        for h in range(4, NH):
            background += head_projection(Q, h) + head_projection(K, h)
        for ub in range(TB):
            background += values_projection(1, ub)
        rate = len(background) // (STEPS - MB)
        shares = [[0, 1, 2, 3], [4, 5], [6, 7]]
        MERGED = 3
        second_share = []
        for m in range(MB - MERGED):
            second_share += output_share(m, shares[1])

        for n in range(STEPS + FLIP_LAG):
            h, tb = divmod(n, TB)
            if 0 <= n - EXP_LAG < STEPS:
                exponentials(n - EXP_LAG)
            if n < STEPS:
                scores_and_max(n)
            if 0 <= n - SCALE_LAG < STEPS:
                scale(n - SCALE_LAG)
            if h + 1 < NH:
                if tb == 0:
                    scalars(h + 1)
                if tb == 1:
                    query_side(h + 1)
                if tb == 2:
                    key_side(h + 1)
            filler = background[n * rate:(n + 1) * rate]
            if STEPS - MB <= n < STEPS:
                filler = filler + output_share(n - (STEPS - MB), shares[0])
            if n >= STEPS:
                filler = filler + second_share[(n - STEPS) * len(second_share) // FLIP_LAG:(n - STEPS + 1) * len(second_share) // FLIP_LAG]
            if 0 <= n - FLIP_LAG < STEPS:
                flip(n - FLIP_LAG, [filler[ub * len(filler) // TB:(ub + 1) * len(filler) // TB] for ub in range(TB)])
            else:
                issue(filler)
            if n >= VALUES_LAG and (n - VALUES_LAG) % TB == 0:
                meet_values((n - VALUES_LAG) // TB)

        OPEN_EARLY = 2
        last_share = [output_share(m, shares[2] if m < MB - MERGED else shares[1] + shares[2]) for m in range(MB)]
        for m in range(OPEN_EARLY):
            issue(last_share[m][:-1])
        meet_values(NH - 1)
        for m in range(OPEN_EARLY, MB - MERGED):
            issue(last_share[m][:-1])
        waiting = []
        for m in range(MB - MERGED, MB):
            waiting += last_share[m][:-1]
        for m in range(MB):
            issue(last_share[m][-1:])
            queue = nc.sync if m % 2 == 0 else nc.scalar
            queue.dma_start(out[m * P:(m + 1) * P, :], out_sb[m][:])
            issue(waiting[m * len(waiting) // (MB - 1):(m + 1) * len(waiting) // (MB - 1)])
